import numpy as np
import ml_dtypes


def mxq(x, axis, fmt="e4m3"):
    dtype, down = {"e4m3": (ml_dtypes.float8_e4m3fn, 7), "e5m2": (ml_dtypes.float8_e5m2, 14)}[fmt]
    v = np.moveaxis(np.asarray(x, np.float32).astype(ml_dtypes.bfloat16).astype(np.float64), axis, -1)
    blocks = v.reshape(v.shape[:-1] + (-1, 32))
    amax = np.abs(blocks).max(-1, keepdims=True)
    byte = np.maximum(np.where(amax > 0, np.frexp(amax)[1] - 1 + 127, 0) - down, 1)
    scale = np.exp2(byte - 127.0)
    codes = (blocks / scale).astype(np.float32).astype(dtype).astype(np.float64)
    return np.moveaxis((codes * scale).reshape(v.shape), -1, axis)


WIDE = False


def mx_kscale(k):
    if not WIDE:
        return np.ones(k)
    levels = np.array([10, -10, 5, -5, 0])
    a = np.random.permutation(np.resize(levels, k // 512 * 4)).reshape(k // 512, 4)
    idx = np.arange(k)
    return np.exp2(a[idx // 512, idx % 128 // 32])


BF16 = ml_dtypes.bfloat16


def bf(x):
    return np.asarray(x, np.float32).astype(BF16)


def f64(x):
    return np.asarray(x).astype(np.float64)


E2M1 = np.array([0.0, 0.5, 1.0, 1.5, 2.0, 3.0, 4.0, 6.0, -0.0, -0.5, -1.0, -1.5, -2.0, -3.0, -4.0, -6.0])


def pack_weight(w, fmt):
    k, n = w.shape
    w = f64(bf(w)).reshape(k // 32, 32, n)
    amax = np.abs(w).max(1)
    if fmt == "e4m3":
        byte = np.frexp(amax)[1] - 1 + 127 - 7
    else:
        mant, ex = np.frexp(amax / 6.0)
        byte = np.where(mant > 0.5, ex, ex - 1) + 127
    byte = np.clip(np.where(amax > 0, byte, 1), 1, 254)
    scaled = (w * np.exp2(127.0 - byte)[:, None, :]).reshape(k, n).astype(np.float32)
    by_word = np.ascontiguousarray(scaled.reshape(k // 512, 128, 4, n).transpose(0, 1, 3, 2))
    if fmt == "e4m3":
        words = by_word.astype(ml_dtypes.float8_e4m3fn).view(np.uint8)
    else:
        c = by_word.astype(ml_dtypes.float4_e2m1fn).view(np.uint8) & 0xF
        words = c[..., 0::2] | (c[..., 1::2] << 4)
    return np.ascontiguousarray(words), np.ascontiguousarray(byte.astype(np.uint8).reshape(k // 512, 16, n))


def unpack_weight(words, scales, fmt):
    g, p, n, _ = words.shape
    if fmt == "e4m3":
        vals = np.ascontiguousarray(words).view(ml_dtypes.float8_e4m3fn).astype(np.float64)
    else:
        nib = np.empty((g, p, n, 4), np.uint8)
        nib[..., 0::2] = words & 0xF
        nib[..., 1::2] = words >> 4
        vals = E2M1[nib]
    vals = vals * np.repeat(np.exp2(scales.astype(np.float64) - 127.0), 8, axis=1)[..., None]
    return vals.transpose(0, 1, 3, 2).reshape(g * 512, n)


B, N, D, P, C = 2, 64, 2048, 256, 3
G = 11 + C
O = P * G
OFFSET_MAX = 0.2
SCALE_MAX = 0.02
FMT = "e4m3"


def sigmoid(v):
    return 1.0 / (1.0 + np.exp(-v))


def silu(v):
    return v / (1.0 + np.exp(-v))


def setup_inputs():
    s = mx_kscale(D)
    xyzs = bf(np.random.standard_normal((B, N, 3)) * 0.25)
    latents = bf(np.random.standard_normal((B, N, D)) * s)
    W1_words, W1_scales = pack_weight(np.random.standard_normal((D, O)) / np.sqrt(D) / s[:, None], FMT)
    b1 = bf(np.random.standard_normal(O) * 0.3)
    W2_words, W2_scales = pack_weight(np.random.standard_normal((O, O)) * 2.5 / np.sqrt(O), FMT)
    b2 = bf(np.random.standard_normal(O) * 0.5)
    return {"xyzs": xyzs,
            "latents": latents,
            "W1_words": W1_words,
            "W1_scales": W1_scales,
            "b1": b1,
            "W2_words": W2_words,
            "W2_scales": W2_scales,
            "b2": b2}


def reference(xyzs, latents, W1_words, W1_scales, b1, W2_words, W2_scales, b2):
    xyzs = f64(xyzs)
    h = silu((mxq(f64(latents), 2, "e4m3") @ unpack_weight(W1_words, W1_scales, FMT)) + f64(b1))
    f = (mxq(h, 2, "e4m3") @ unpack_weight(W2_words, W2_scales, FMT)) + f64(b2)
    f = f.reshape(B, N, P, G)
    mean3D = xyzs[:, :, None, :] + sigmoid(f[..., 0:3]) * OFFSET_MAX
    opacity = sigmoid(f[..., 3:4])
    scales = sigmoid(f[..., 4:7]) * SCALE_MAX
    rot = f[..., 7:11]
    rot = rot / np.maximum(np.sqrt(np.sum(rot * rot, axis=-1, keepdims=True)), 1e-12)
    rgb = np.clip(f[..., 11:], -0.5, 0.5) + 0.5
    gaussians = np.concatenate([mean3D, opacity, scales, rot, rgb], axis=-1)
    return gaussians.reshape(B, N * P, G)

@@ -1,0 +1,263 @@
+from contextlib import ExitStack
+
+import concourse.mybir as mybir
+from concourse.masks import make_identity
+
+F32 = mybir.dt.float32
+BF16 = mybir.dt.bfloat16
+I32 = mybir.dt.int32
+U32 = mybir.dt.uint32
+U8 = mybir.dt.uint8
+FP8X4 = mybir.dt.float8_e4m3fn_x4
+ALU = mybir.AluOpType
+ACT = mybir.ActivationFunctionType
+AX = mybir.AxisListType
+
+P = 128
+D = 2048
+O = 3584
+CH = 14
+BANK = 512
+G1 = D // 512
+G2 = O // 512
+NB = O // BANK
+
+PHASES = ((0, 1024), (1024, 2048), (2048, 3072), (3072, 3584))
+GAUSS_END = (72, 144, 216, 256)
+
+FLOPS = 2 * P * (D * O + O * O)
+
+
+def tile_gaussianrenderer_w_kernel(tc, xyzs, latents, W1_words, W1_scales, b1, W2_words, W2_scales, b2, out):
+    nc = tc.nc
+    with ExitStack() as ctx:
+        const = ctx.enter_context(tc.tile_pool(name="const", bufs=1))
+        big = ctx.enter_context(tc.tile_pool(name="big", bufs=4))
+        w2pool = ctx.enter_context(tc.tile_pool(name="w2pool", bufs=1))
+        opool = ctx.enter_context(tc.tile_pool(name="opool", bufs=1))
+        work = ctx.enter_context(tc.tile_pool(name="work", bufs=2))
+        psum = ctx.enter_context(tc.psum_pool(name="psum", bufs=8))
+        ctx.enter_context(tc.manual_schedule())
+
+        bias_rows = const.tile([P, BANK], BF16, name="bias_rows")
+        planes1 = const.tile([P, O], U8, name="planes1", align_bytes=64)
+        planes2a = const.tile([P, O], U8, name="planes2a", align_bytes=64)
+        planes2b = const.tile([P, O], U8, name="planes2b", align_bytes=64)
+        nc.vector.memset(bias_rows[:].bitcast(I32), 0)
+        nc.vector.memset(planes1[:].bitcast(I32), 0)
+        nc.vector.memset(planes2a[:].bitcast(I32), 0)
+        nc.vector.memset(planes2b[:].bitcast(I32), 0)
+
+        ident_bf = const.tile([P, P], BF16, name="ident_bf")
+        make_identity(nc, ident_bf[:])
+        ident_f = const.tile([P, P], F32, name="ident_f")
+        make_identity(nc, ident_f[:])
+
+        xyz_bf = const.tile([P, 3], BF16, name="xyz_bf")
+        nc.scalar.dma_start(out=xyz_bf[:], in_=xyzs.flatten_outer_dims())
+        nc.scalar.dma_start(out=bias_rows[0:NB, :], in_=b1.rearrange("(j c) -> j c", c=BANK))
+        nc.scalar.dma_start(out=bias_rows[NB : 2 * NB, :], in_=b2.rearrange("(j c) -> j c", c=BANK))
+
+        x_sb = const.tile([P, D], BF16, name="x_sb")
+        nc.sync.dma_start(out=x_sb[:], in_=latents.flatten_outer_dims())
+        for q in range(4):
+            nc.sync.dma_start(
+                out=planes1[32 * q : 32 * q + 16, :].bitcast(I32),
+                in_=W1_scales[:, 4 * q : 4 * q + 4, :].bitcast(I32),
+            )
+        for q in range(4):
+            nc.sync.dma_start(
+                out=planes2a[32 * q : 32 * q + 16, :].bitcast(I32),
+                in_=W2_scales[0:4, 4 * q : 4 * q + 4, :].bitcast(I32),
+            )
+        for q in range(4):
+            nc.sync.dma_start(
+                out=planes2b[32 * q : 32 * q + 12, :].bitcast(I32),
+                in_=W2_scales[4:7, 4 * q : 4 * q + 4, :].bitcast(I32),
+            )
+        w1 = []
+        for g in range(G1):
+            w1_t = big.tile([P, O], U32, name="w1_%d" % g, tag="big", align_bytes=64)
+            nc.sync.dma_start(out=w1_t[:].bitcast(I32), in_=W1_words[g].rearrange("p n t -> p (n t)").bitcast(I32))
+            w1.append(w1_t)
+        w2 = []
+        for ph, (c0, c1) in enumerate(PHASES):
+            row = []
+            for g in range(G2):
+                w2_t = w2pool.tile([P, c1 - c0], U32, name="w2_%d_%d" % (ph, g), align_bytes=64)
+                nc.sync.dma_start(
+                    out=w2_t[:].bitcast(I32),
+                    in_=W2_words[g, :, c0:c1, :].rearrange("p n t -> p (n t)").bitcast(I32),
+                )
+                row.append(w2_t)
+            w2.append(row)
+
+        xyz_f = const.tile([P, 3], F32, name="xyz_f")
+        nc.vector.tensor_copy(out=xyz_f[:], in_=xyz_bf[:])
+
+        b1p = const.tile([P, NB, 4, P], BF16, name="b1p")
+        for j in range(NB):
+            pb = psum.tile([P, BANK], F32, name="pb1", tag="ps")
+            nc.tensor.matmul(
+                out=pb[:], lhsT=ident_bf[:, j : j + 1].to_broadcast([P, P]), rhs=bias_rows[:], start=True, stop=True
+            )
+            nc.scalar.copy(out=b1p[:, j, :, :], in_=pb[:].rearrange("p (q t) -> p t q", t=4))
+
+        xw = x_sb[:].bitcast(F32)
+        xg = const.tile([P, D], BF16, name="xg", align_bytes=64)
+        xgw = xg[:].bitcast(F32).rearrange("p (g r u) -> p g r u", g=G1, u=2)
+        for half in range(2):
+            xt = psum.tile([P, 2, 2, P], F32, name="xt", tag="ps")
+            for g2 in range(2):
+                g = 2 * half + g2
+                for u in range(2):
+                    nc.tensor.transpose(xt[:, g2, u, :], xw[:, 256 * g + u : 256 * (g + 1) : 2], ident_f[:])
+            nc.vector.tensor_copy(out=xgw[:, 2 * half : 2 * half + 2, :, :], in_=xt[:].rearrange("p g u r -> p g r u"))
+        xcodes = const.tile([P, G1 * P], U32, name="xcodes", align_bytes=64)
+        xplane = const.tile([P, G1 * P], U8, name="xplane", align_bytes=64)
+        nc.vector.quantize_mx(out=xcodes[:].bitcast(FP8X4), scales=xplane[:], in_=xg[:])
+
+        b2b = const.tile([P, O], F32, name="b2b")
+        for j in range(NB):
+            pb = psum.tile([P, BANK], F32, name="pb2", tag="ps")
+            nc.tensor.matmul(
+                out=pb[:],
+                lhsT=ident_bf[:, NB + j : NB + j + 1].to_broadcast([P, P]),
+                rhs=bias_rows[:],
+                start=True,
+                stop=True,
+            )
+            nc.vector.tensor_copy(out=b2b[:, BANK * j : BANK * (j + 1)], in_=pb[:])
+        b2v = b2b[:].rearrange("p (n c) -> p n c", c=CH)
+        nc.gpsimd.tensor_scalar(
+            out=b2v[:, :, 11:14], in0=b2v[:, :, 11:14], scalar1=1.0, scalar2=0.5, op0=ALU.mult, op1=ALU.add
+        )
+
+        ps1 = []
+        for j in range(NB):
+            ps1_t = psum.tile([P, BANK], F32, name="ps1_%d" % j, tag="ps")
+            ps1.append(ps1_t)
+        for g in range(G1):
+            for j in range(NB):
+                nc.tensor.matmul_mx(
+                    out=ps1[j][:],
+                    lhsT=xcodes[:, P * g : P * (g + 1)].bitcast(FP8X4),
+                    lhsT_scale=xplane[:, P * g : P * (g + 1)],
+                    rhs=w1[g][:, BANK * j : BANK * (j + 1)].bitcast(FP8X4),
+                    rhs_scale=planes1[4 * g : P, BANK * j : BANK * (j + 1)],
+                    start=(g == 0),
+                    stop=(g == G1 - 1),
+                )
+
+        h_sb = big.tile([P, NB, BANK], BF16, name="h_sb", tag="big", align_bytes=64)
+        hg = big.tile([P, NB, BANK], BF16, name="hg", tag="big", align_bytes=64)
+        hcodes = []
+        hplane = []
+        for j in range(NB):
+            hc_t = const.tile([P, P], U32, name="hcodes_%d" % j, align_bytes=64)
+            hp_t = const.tile([P, P], U8, name="hplane_%d" % j, align_bytes=64)
+            hcodes.append(hc_t)
+            hplane.append(hp_t)
+
+        def h_value(j):
+            tmp = work.tile([P, 4, P], F32, name="tmp", bufs=3)
+            nc.vector.tensor_tensor(
+                out=tmp[:], in0=ps1[j][:].rearrange("p (q t) -> p t q", t=4), in1=b1p[:, j, :, :], op=ALU.add
+            )
+            nc.scalar.activation(out=h_sb[:, j, :], in_=tmp[:].rearrange("p t q -> p (t q)"), func=ACT.Silu)
+
+        def h_turn(j):
+            ht = psum.tile([P, 4, P], BF16, name="ht", tag="ps")
+            for t in range(4):
+                nc.tensor.transpose(ht[:, t, :], h_sb[:, j, P * t : P * (t + 1)], ident_bf[:])
+            dst = hg[:, j, :].rearrange("p (r t) -> p r t", t=4)
+            src = ht[:].rearrange("p t r -> p r t")
+            if j % 2 == 0:
+                nc.vector.tensor_copy(out=dst, in_=src)
+            else:
+                nc.scalar.copy(out=dst, in_=src)
+
+        def h_quant(j):
+            nc.vector.quantize_mx(out=hcodes[j][:].bitcast(FP8X4), scales=hplane[j][:], in_=hg[:, j, :])
+
+        for s in range(NB + 3):
+            if s < NB:
+                h_value(s)
+            if 0 <= s - 2 < NB:
+                h_turn(s - 2)
+            if 0 <= s - 3 < NB:
+                h_quant(s - 3)
+
+        out_v = out.rearrange("b (n p) c -> (b n) (p c)", p=256)
+        o_tiles = []
+        g_start = []
+        for ph in range(len(PHASES)):
+            gs = 0 if ph == 0 else GAUSS_END[ph - 1]
+            o_t = opool.tile([P, GAUSS_END[ph] - gs, CH], F32, name="o_%d" % ph)
+            o_tiles.append(o_t)
+            g_start.append(gs)
+
+        for ph, (c0, c1) in enumerate(PHASES):
+            nbank = (c1 - c0) // BANK
+            acc = []
+            for b in range(nbank):
+                acc_t = psum.tile([P, BANK], F32, name="acc_%d_%d" % (ph, b), tag="ps")
+                acc.append(acc_t)
+            for g in range(G2):
+                planes = planes2a if g < 4 else planes2b
+                k = 4 * (g % 4)
+                for b in range(nbank):
+                    nc.tensor.matmul_mx(
+                        out=acc[b][:],
+                        lhsT=hcodes[g][:].bitcast(FP8X4),
+                        lhsT_scale=hplane[g][:],
+                        rhs=w2[ph][g][:, BANK * b : BANK * (b + 1)].bitcast(FP8X4),
+                        rhs_scale=planes[k:P, c0 + BANK * b : c0 + BANK * (b + 1)],
+                        start=(g == 0),
+                        stop=(g == G2 - 1),
+                    )
+            for b in range(nbank):
+                lo = c0 + BANK * b
+                hi = lo + BANK
+                cut = CH * GAUSS_END[ph]
+                pieces = [(lo, hi, ph)] if hi <= cut else [(lo, cut, ph), (cut, hi, ph + 1)]
+                for a, e, tph in pieces:
+                    off = CH * g_start[tph]
+                    nc.vector.tensor_tensor(
+                        out=o_tiles[tph][:].rearrange("p n c -> p (n c)")[:, a - off : e - off],
+                        in0=acc[b][:, a - lo : e - lo],
+                        in1=b2b[:, a:e],
+                        op=ALU.add,
+                    )
+            o = o_tiles[ph]
+            ng = GAUSS_END[ph] - g_start[ph]
+            nc.scalar.activation(out=o[:, :, 0:7], in_=o[:, :, 0:7], func=ACT.Sigmoid)
+            sq = work.tile([P, ng, 4], F32, name="sq")
+            nc.vector.tensor_tensor(out=sq[:], in0=o[:, :, 7:11], in1=o[:, :, 7:11], op=ALU.mult)
+            ss = work.tile([P, ng], F32, name="ss")
+            nc.vector.tensor_reduce(out=ss[:], in_=sq[:], axis=AX.X, op=ALU.add)
+            rinv = work.tile([P, ng], F32, name="rinv")
+            nc.scalar.activation(out=rinv[:], in_=ss[:], func=ACT.Abs_reciprocal_sqrt)
+            nc.vector.scalar_tensor_tensor(
+                out=o[:, :, 0:3],
+                in0=o[:, :, 0:3],
+                scalar=0.2,
+                in1=xyz_f[:].unsqueeze(1).to_broadcast([P, ng, 3]),
+                op0=ALU.mult,
+                op1=ALU.add,
+            )
+            nc.vector.tensor_scalar(out=o[:, :, 4:7], in0=o[:, :, 4:7], scalar1=0.02, scalar2=None, op0=ALU.mult)
+            nc.vector.tensor_scalar(
+                out=o[:, :, 11:14], in0=o[:, :, 11:14], scalar1=0.0, scalar2=1.0, op0=ALU.max, op1=ALU.min
+            )
+            nc.vector.scalar_tensor_tensor(
+                out=o[:, :, 7:11],
+                in0=rinv[:].unsqueeze(2).to_broadcast([P, ng, 4]),
+                scalar=1.0e12,
+                in1=o[:, :, 7:11],
+                op0=ALU.min,
+                op1=ALU.mult,
+            )
+            nc.sync.dma_start(
+                out=out_v[:, CH * g_start[ph] : CH * GAUSS_END[ph]], in_=o[:].rearrange("p n c -> p (n c)")
+            )

@@ -61,19 +61,19 @@ def tile_gaussianrenderer_w_kernel(tc, xyzs, latents, W1_words, W1_scales, b1, W
         x_sb = const.tile([P, D], BF16, name="x_sb")
         nc.sync.dma_start(out=x_sb[:], in_=latents.flatten_outer_dims())
         for q in range(4):
-            nc.sync.dma_start(
-                out=planes1[32 * q : 32 * q + 16, :].bitcast(I32),
-                in_=W1_scales[:, 4 * q : 4 * q + 4, :].bitcast(I32),
+            nc.gpsimd.dma_start(
+                out=planes1[32 * q : 32 * q + 16, :].bitcast(F32),
+                in_=W1_scales[:, 4 * q : 4 * q + 4, :].bitcast(F32),
             )
         for q in range(4):
-            nc.sync.dma_start(
-                out=planes2a[32 * q : 32 * q + 16, :].bitcast(I32),
-                in_=W2_scales[0:4, 4 * q : 4 * q + 4, :].bitcast(I32),
+            nc.gpsimd.dma_start(
+                out=planes2a[32 * q : 32 * q + 16, :].bitcast(F32),
+                in_=W2_scales[0:4, 4 * q : 4 * q + 4, :].bitcast(F32),
             )
         for q in range(4):
-            nc.sync.dma_start(
-                out=planes2b[32 * q : 32 * q + 12, :].bitcast(I32),
-                in_=W2_scales[4:7, 4 * q : 4 * q + 4, :].bitcast(I32),
+            nc.gpsimd.dma_start(
+                out=planes2b[32 * q : 32 * q + 12, :].bitcast(F32),
+                in_=W2_scales[4:7, 4 * q : 4 * q + 4, :].bitcast(F32),
             )
         w1 = []
         for g in range(G1):

@@ -22,8 +22,8 @@ G1 = D // 512
 G2 = O // 512
 NB = O // BANK
 
-PHASES = ((0, 1024), (1024, 2048), (2048, 3072), (3072, 3584))
-GAUSS_END = (72, 144, 216, 256)
+PHASES = ((0, 1280), (1280, 2304), (2304, 3072), (3072, 3584))
+GAUSS_END = (88, 164, 216, 256)
 
 FLOPS = 2 * P * (D * O + O * O)
 
@@ -197,29 +197,44 @@ def tile_gaussianrenderer_w_kernel(tc, xyzs, latents, W1_words, W1_scales, b1, W
             o_tiles.append(o_t)
             g_start.append(gs)
 
+        rinvs = []
+
+        def norm_and_store(ph):
+            o = o_tiles[ph]
+            ng = GAUSS_END[ph] - g_start[ph]
+            nc.vector.scalar_tensor_tensor(
+                out=o[:, :, 7:11],
+                in0=rinvs[ph][:].unsqueeze(2).to_broadcast([P, ng, 4]),
+                scalar=1.0e12,
+                in1=o[:, :, 7:11],
+                op0=ALU.min,
+                op1=ALU.mult,
+            )
+            nc.sync.dma_start(
+                out=out_v[:, CH * g_start[ph] : CH * GAUSS_END[ph]], in_=o[:].rearrange("p n c -> p (n c)")
+            )
+
         for ph, (c0, c1) in enumerate(PHASES):
-            nbank = (c1 - c0) // BANK
+            banks = [(lo, min(lo + BANK, c1)) for lo in range(c0, c1, BANK)]
             acc = []
-            for b in range(nbank):
-                acc_t = psum.tile([P, BANK], F32, name="acc_%d_%d" % (ph, b), tag="ps")
+            for lo, hi in banks:
+                acc_t = psum.tile([P, hi - lo], F32, name="acc_%d" % lo, tag="ps")
                 acc.append(acc_t)
             for g in range(G2):
                 planes = planes2a if g < 4 else planes2b
                 k = 4 * (g % 4)
-                for b in range(nbank):
+                for b, (lo, hi) in enumerate(banks):
                     nc.tensor.matmul_mx(
                         out=acc[b][:],
                         lhsT=hcodes[g][:].bitcast(FP8X4),
                         lhsT_scale=hplane[g][:],
-                        rhs=w2[ph][g][:, BANK * b : BANK * (b + 1)].bitcast(FP8X4),
-                        rhs_scale=planes[k:P, c0 + BANK * b : c0 + BANK * (b + 1)],
+                        rhs=w2[ph][g][:, lo - c0 : hi - c0].bitcast(FP8X4),
+                        rhs_scale=planes[k:P, lo:hi],
                         start=(g == 0),
                         stop=(g == G2 - 1),
                     )
-            for b in range(nbank):
-                lo = c0 + BANK * b
-                hi = lo + BANK
-                cut = CH * GAUSS_END[ph]
+            cut = CH * GAUSS_END[ph]
+            for b, (lo, hi) in enumerate(banks):
                 pieces = [(lo, hi, ph)] if hi <= cut else [(lo, cut, ph), (cut, hi, ph + 1)]
                 for a, e, tph in pieces:
                     off = CH * g_start[tph]
@@ -234,10 +249,16 @@ def tile_gaussianrenderer_w_kernel(tc, xyzs, latents, W1_words, W1_scales, b1, W
             nc.scalar.activation(out=o[:, :, 0:7], in_=o[:, :, 0:7], func=ACT.Sigmoid)
             sq = work.tile([P, ng, 4], F32, name="sq")
             nc.vector.tensor_tensor(out=sq[:], in0=o[:, :, 7:11], in1=o[:, :, 7:11], op=ALU.mult)
+            nc.vector.tensor_scalar(
+                out=o[:, :, 11:14], in0=o[:, :, 11:14], scalar1=0.0, scalar2=1.0, op0=ALU.max, op1=ALU.min
+            )
             ss = work.tile([P, ng], F32, name="ss")
             nc.vector.tensor_reduce(out=ss[:], in_=sq[:], axis=AX.X, op=ALU.add)
             rinv = work.tile([P, ng], F32, name="rinv")
+            rinvs.append(rinv)
             nc.scalar.activation(out=rinv[:], in_=ss[:], func=ACT.Abs_reciprocal_sqrt)
+            if ph > 0:
+                norm_and_store(ph - 1)
             nc.vector.scalar_tensor_tensor(
                 out=o[:, :, 0:3],
                 in0=o[:, :, 0:3],
@@ -247,17 +268,4 @@ def tile_gaussianrenderer_w_kernel(tc, xyzs, latents, W1_words, W1_scales, b1, W
                 op1=ALU.add,
             )
             nc.vector.tensor_scalar(out=o[:, :, 4:7], in0=o[:, :, 4:7], scalar1=0.02, scalar2=None, op0=ALU.mult)
-            nc.vector.tensor_scalar(
-                out=o[:, :, 11:14], in0=o[:, :, 11:14], scalar1=0.0, scalar2=1.0, op0=ALU.max, op1=ALU.min
-            )
-            nc.vector.scalar_tensor_tensor(
-                out=o[:, :, 7:11],
-                in0=rinv[:].unsqueeze(2).to_broadcast([P, ng, 4]),
-                scalar=1.0e12,
-                in1=o[:, :, 7:11],
-                op0=ALU.min,
-                op1=ALU.mult,
-            )
-            nc.sync.dma_start(
-                out=out_v[:, CH * g_start[ph] : CH * GAUSS_END[ph]], in_=o[:].rearrange("p n c -> p (n c)")
-            )
+        norm_and_store(len(PHASES) - 1)

@@ -22,8 +22,8 @@ G1 = D // 512
 G2 = O // 512
 NB = O // BANK
 
-PHASES = ((0, 1280), (1280, 2304), (2304, 3072), (3072, 3584))
-GAUSS_END = (88, 164, 216, 256)
+PHASES = ((0, 1792), (1792, 2688), (2688, 3200), (3200, 3584))
+GAUSS_END = (128, 192, 228, 256)
 
 FLOPS = 2 * P * (D * O + O * O)
 
@@ -197,25 +197,17 @@ def tile_gaussianrenderer_w_kernel(tc, xyzs, latents, W1_words, W1_scales, b1, W
             o_tiles.append(o_t)
             g_start.append(gs)
 
-        rinvs = []
+        ss = const.tile([P, 256], F32, name="ss")
+        rinv = const.tile([P, 256], F32, name="rinv")
 
-        def norm_and_store(ph):
-            o = o_tiles[ph]
-            ng = GAUSS_END[ph] - g_start[ph]
-            nc.vector.scalar_tensor_tensor(
-                out=o[:, :, 7:11],
-                in0=rinvs[ph][:].unsqueeze(2).to_broadcast([P, ng, 4]),
-                scalar=1.0e12,
-                in1=o[:, :, 7:11],
-                op0=ALU.min,
-                op1=ALU.mult,
-            )
-            nc.sync.dma_start(
-                out=out_v[:, CH * g_start[ph] : CH * GAUSS_END[ph]], in_=o[:].rearrange("p n c -> p (n c)")
-            )
-
-        for ph, (c0, c1) in enumerate(PHASES):
-            banks = [(lo, min(lo + BANK, c1)) for lo in range(c0, c1, BANK)]
+        def matmuls_and_bias(ph):
+            c0, c1 = PHASES[ph]
+            banks = []
+            lo = c0
+            while lo < c1:
+                hi = lo + max(n for n in (128, 256, BANK) if lo + n <= c1)
+                banks.append((lo, hi))
+                lo = hi
             acc = []
             for lo, hi in banks:
                 acc_t = psum.tile([P, hi - lo], F32, name="acc_%d" % lo, tag="ps")
@@ -244,28 +236,72 @@ def tile_gaussianrenderer_w_kernel(tc, xyzs, latents, W1_words, W1_scales, b1, W
                         in1=b2b[:, a:e],
                         op=ALU.add,
                     )
+
+        def sigmoid(ph):
             o = o_tiles[ph]
-            ng = GAUSS_END[ph] - g_start[ph]
             nc.scalar.activation(out=o[:, :, 0:7], in_=o[:, :, 0:7], func=ACT.Sigmoid)
-            sq = work.tile([P, ng, 4], F32, name="sq")
+
+        def square_sum_and_clip(ph):
+            o = o_tiles[ph]
+            sq = work.tile([P, GAUSS_END[ph] - g_start[ph], 4], F32, name="sq")
             nc.vector.tensor_tensor(out=sq[:], in0=o[:, :, 7:11], in1=o[:, :, 7:11], op=ALU.mult)
+            nc.vector.tensor_reduce(out=ss[:, g_start[ph] : GAUSS_END[ph]], in_=sq[:], axis=AX.X, op=ALU.add)
             nc.vector.tensor_scalar(
                 out=o[:, :, 11:14], in0=o[:, :, 11:14], scalar1=0.0, scalar2=1.0, op0=ALU.max, op1=ALU.min
             )
-            ss = work.tile([P, ng], F32, name="ss")
-            nc.vector.tensor_reduce(out=ss[:], in_=sq[:], axis=AX.X, op=ALU.add)
-            rinv = work.tile([P, ng], F32, name="rinv")
-            rinvs.append(rinv)
-            nc.scalar.activation(out=rinv[:], in_=ss[:], func=ACT.Abs_reciprocal_sqrt)
-            if ph > 0:
-                norm_and_store(ph - 1)
+
+        def inverse_norm(first, last):
+            cols = slice(g_start[first], GAUSS_END[last])
+            nc.scalar.activation(out=rinv[:, cols], in_=ss[:, cols], func=ACT.Abs_reciprocal_sqrt)
+
+        def means_and_sizes(ph):
+            o = o_tiles[ph]
             nc.vector.scalar_tensor_tensor(
                 out=o[:, :, 0:3],
                 in0=o[:, :, 0:3],
                 scalar=0.2,
-                in1=xyz_f[:].unsqueeze(1).to_broadcast([P, ng, 3]),
+                in1=xyz_f[:].unsqueeze(1).to_broadcast([P, GAUSS_END[ph] - g_start[ph], 3]),
                 op0=ALU.mult,
                 op1=ALU.add,
             )
             nc.vector.tensor_scalar(out=o[:, :, 4:7], in0=o[:, :, 4:7], scalar1=0.02, scalar2=None, op0=ALU.mult)
-        norm_and_store(len(PHASES) - 1)
+
+        def norm_and_store(ph):
+            o = o_tiles[ph]
+            n0, n1 = g_start[ph], GAUSS_END[ph]
+            nc.vector.scalar_tensor_tensor(
+                out=o[:, :, 7:11],
+                in0=rinv[:, n0:n1].unsqueeze(2).to_broadcast([P, n1 - n0, 4]),
+                scalar=1.0e12,
+                in1=o[:, :, 7:11],
+                op0=ALU.min,
+                op1=ALU.mult,
+            )
+            nc.sync.dma_start(out=out_v[:, CH * n0 : CH * n1], in_=o[:].rearrange("p n c -> p (n c)"))
+
+        matmuls_and_bias(0)
+        sigmoid(0)
+        square_sum_and_clip(0)
+        inverse_norm(0, 0)
+        means_and_sizes(0)
+
+        matmuls_and_bias(1)
+        sigmoid(1)
+        square_sum_and_clip(1)
+        inverse_norm(1, 1)
+        norm_and_store(0)
+        means_and_sizes(1)
+
+        matmuls_and_bias(2)
+        sigmoid(2)
+        square_sum_and_clip(2)
+        norm_and_store(1)
+
+        matmuls_and_bias(3)
+        sigmoid(3)
+        square_sum_and_clip(3)
+        inverse_norm(2, 3)
+        means_and_sizes(2)
+        means_and_sizes(3)
+        norm_and_store(2)
+        norm_and_store(3)

@@ -25,6 +25,8 @@ NB = O // BANK
 PHASES = ((0, 1792), (1792, 2688), (2688, 3200), (3200, 3584))
 GAUSS_END = (128, 192, 228, 256)
 
+LEAD = 1
+
 FLOPS = 2 * P * (D * O + O * O)
 
 
@@ -193,8 +195,9 @@ def tile_gaussianrenderer_w_kernel(tc, xyzs, latents, W1_words, W1_scales, b1, W
         g_start = []
         for ph in range(len(PHASES)):
             gs = 0 if ph == 0 else GAUSS_END[ph - 1]
-            o_t = opool.tile([P, GAUSS_END[ph] - gs, CH], F32, name="o_%d" % ph)
-            o_tiles.append(o_t)
+            width = CH * (GAUSS_END[ph] - gs)
+            o_t = opool.tile([P, LEAD + width], F32, name="o_%d" % ph, align_bytes=64)
+            o_tiles.append(o_t[:, LEAD : LEAD + width].rearrange("p (n c) -> p n c", c=CH))
             g_start.append(gs)
 
         ss = const.tile([P, 256], F32, name="ss")
@@ -231,7 +234,7 @@ def tile_gaussianrenderer_w_kernel(tc, xyzs, latents, W1_words, W1_scales, b1, W
                 for a, e, tph in pieces:
                     off = CH * g_start[tph]
                     nc.vector.tensor_tensor(
-                        out=o_tiles[tph][:].rearrange("p n c -> p (n c)")[:, a - off : e - off],
+                        out=o_tiles[tph].rearrange("p n c -> p (n c)")[:, a - off : e - off],
                         in0=acc[b][:, a - lo : e - lo],
                         in1=b2b[:, a:e],
                         op=ALU.add,
@@ -277,7 +280,7 @@ def tile_gaussianrenderer_w_kernel(tc, xyzs, latents, W1_words, W1_scales, b1, W
                 op0=ALU.min,
                 op1=ALU.mult,
             )
-            nc.sync.dma_start(out=out_v[:, CH * n0 : CH * n1], in_=o[:].rearrange("p n c -> p (n c)"))
+            nc.sync.dma_start(out=out_v[:, CH * n0 : CH * n1], in_=o.rearrange("p n c -> p (n c)"))
 
         matmuls_and_bias(0)
         sigmoid(0)

from contextlib import ExitStack

import concourse.mybir as mybir
from concourse.masks import make_identity

F32 = mybir.dt.float32
BF16 = mybir.dt.bfloat16
I32 = mybir.dt.int32
U32 = mybir.dt.uint32
U8 = mybir.dt.uint8
FP8X4 = mybir.dt.float8_e4m3fn_x4
ALU = mybir.AluOpType
ACT = mybir.ActivationFunctionType
AX = mybir.AxisListType

P = 128
D = 2048
O = 3584
CH = 14
BANK = 512
G1 = D // 512
G2 = O // 512
NB = O // BANK

PHASES = ((0, 1792), (1792, 2688), (2688, 3200), (3200, 3584))
GAUSS_END = (128, 192, 228, 256)

LEAD = 1

FLOPS = 2 * P * (D * O + O * O)


def tile_gaussianrenderer_w_kernel(tc, xyzs, latents, W1_words, W1_scales, b1, W2_words, W2_scales, b2, out):
    nc = tc.nc
    with ExitStack() as ctx:
        const = ctx.enter_context(tc.tile_pool(name="const", bufs=1))
        big = ctx.enter_context(tc.tile_pool(name="big", bufs=4))
        w2pool = ctx.enter_context(tc.tile_pool(name="w2pool", bufs=1))
        opool = ctx.enter_context(tc.tile_pool(name="opool", bufs=1))
        work = ctx.enter_context(tc.tile_pool(name="work", bufs=2))
        psum = ctx.enter_context(tc.psum_pool(name="psum", bufs=8))
        ctx.enter_context(tc.manual_schedule())

        bias_rows = const.tile([P, BANK], BF16, name="bias_rows")
        planes1 = const.tile([P, O], U8, name="planes1", align_bytes=64)
        planes2a = const.tile([P, O], U8, name="planes2a", align_bytes=64)
        planes2b = const.tile([P, O], U8, name="planes2b", align_bytes=64)
        nc.vector.memset(bias_rows[:].bitcast(I32), 0)
        nc.vector.memset(planes1[:].bitcast(I32), 0)
        nc.vector.memset(planes2a[:].bitcast(I32), 0)
        nc.vector.memset(planes2b[:].bitcast(I32), 0)

        ident_bf = const.tile([P, P], BF16, name="ident_bf")
        make_identity(nc, ident_bf[:])
        ident_f = const.tile([P, P], F32, name="ident_f")
        make_identity(nc, ident_f[:])

        xyz_bf = const.tile([P, 3], BF16, name="xyz_bf")
        nc.scalar.dma_start(out=xyz_bf[:], in_=xyzs.flatten_outer_dims())
        nc.scalar.dma_start(out=bias_rows[0:NB, :], in_=b1.rearrange("(j c) -> j c", c=BANK))
        nc.scalar.dma_start(out=bias_rows[NB : 2 * NB, :], in_=b2.rearrange("(j c) -> j c", c=BANK))

        x_sb = const.tile([P, D], BF16, name="x_sb")
        nc.sync.dma_start(out=x_sb[:], in_=latents.flatten_outer_dims())
        for q in range(4):
            nc.gpsimd.dma_start(
                out=planes1[32 * q : 32 * q + 16, :].bitcast(F32),
                in_=W1_scales[:, 4 * q : 4 * q + 4, :].bitcast(F32),
            )
        for q in range(4):
            nc.gpsimd.dma_start(
                out=planes2a[32 * q : 32 * q + 16, :].bitcast(F32),
                in_=W2_scales[0:4, 4 * q : 4 * q + 4, :].bitcast(F32),
            )
        for q in range(4):
            nc.gpsimd.dma_start(
                out=planes2b[32 * q : 32 * q + 12, :].bitcast(F32),
                in_=W2_scales[4:7, 4 * q : 4 * q + 4, :].bitcast(F32),
            )
        w1 = []
        for g in range(G1):
            w1_t = big.tile([P, O], U32, name="w1_%d" % g, tag="big", align_bytes=64)
            nc.sync.dma_start(out=w1_t[:].bitcast(I32), in_=W1_words[g].rearrange("p n t -> p (n t)").bitcast(I32))
            w1.append(w1_t)
        w2 = []
        for ph, (c0, c1) in enumerate(PHASES):
            row = []
            for g in range(G2):
                w2_t = w2pool.tile([P, c1 - c0], U32, name="w2_%d_%d" % (ph, g), align_bytes=64)
                nc.sync.dma_start(
                    out=w2_t[:].bitcast(I32),
                    in_=W2_words[g, :, c0:c1, :].rearrange("p n t -> p (n t)").bitcast(I32),
                )
                row.append(w2_t)
            w2.append(row)

        xyz_f = const.tile([P, 3], F32, name="xyz_f")
        nc.vector.tensor_copy(out=xyz_f[:], in_=xyz_bf[:])

        b1p = const.tile([P, NB, 4, P], BF16, name="b1p")
        for j in range(NB):
            pb = psum.tile([P, BANK], F32, name="pb1", tag="ps")
            nc.tensor.matmul(
                out=pb[:], lhsT=ident_bf[:, j : j + 1].to_broadcast([P, P]), rhs=bias_rows[:], start=True, stop=True
            )
            nc.scalar.copy(out=b1p[:, j, :, :], in_=pb[:].rearrange("p (q t) -> p t q", t=4))

        xw = x_sb[:].bitcast(F32)
        xg = const.tile([P, D], BF16, name="xg", align_bytes=64)
        xgw = xg[:].bitcast(F32).rearrange("p (g r u) -> p g r u", g=G1, u=2)
        for half in range(2):
            xt = psum.tile([P, 2, 2, P], F32, name="xt", tag="ps")
            for g2 in range(2):
                g = 2 * half + g2
                for u in range(2):
                    nc.tensor.transpose(xt[:, g2, u, :], xw[:, 256 * g + u : 256 * (g + 1) : 2], ident_f[:])
            nc.vector.tensor_copy(out=xgw[:, 2 * half : 2 * half + 2, :, :], in_=xt[:].rearrange("p g u r -> p g r u"))
        xcodes = const.tile([P, G1 * P], U32, name="xcodes", align_bytes=64)
        xplane = const.tile([P, G1 * P], U8, name="xplane", align_bytes=64)
        nc.vector.quantize_mx(out=xcodes[:].bitcast(FP8X4), scales=xplane[:], in_=xg[:])

        b2b = const.tile([P, O], F32, name="b2b")
        for j in range(NB):
            pb = psum.tile([P, BANK], F32, name="pb2", tag="ps")
            nc.tensor.matmul(
                out=pb[:],
                lhsT=ident_bf[:, NB + j : NB + j + 1].to_broadcast([P, P]),
                rhs=bias_rows[:],
                start=True,
                stop=True,
            )
            nc.vector.tensor_copy(out=b2b[:, BANK * j : BANK * (j + 1)], in_=pb[:])
        b2v = b2b[:].rearrange("p (n c) -> p n c", c=CH)
        nc.gpsimd.tensor_scalar(
            out=b2v[:, :, 11:14], in0=b2v[:, :, 11:14], scalar1=1.0, scalar2=0.5, op0=ALU.mult, op1=ALU.add
        )

        ps1 = []
        for j in range(NB):
            ps1_t = psum.tile([P, BANK], F32, name="ps1_%d" % j, tag="ps")
            ps1.append(ps1_t)
        for g in range(G1):
            for j in range(NB):
                nc.tensor.matmul_mx(
                    out=ps1[j][:],
                    lhsT=xcodes[:, P * g : P * (g + 1)].bitcast(FP8X4),
                    lhsT_scale=xplane[:, P * g : P * (g + 1)],
                    rhs=w1[g][:, BANK * j : BANK * (j + 1)].bitcast(FP8X4),
                    rhs_scale=planes1[4 * g : P, BANK * j : BANK * (j + 1)],
                    start=(g == 0),
                    stop=(g == G1 - 1),
                )

        h_sb = big.tile([P, NB, BANK], BF16, name="h_sb", tag="big", align_bytes=64)
        hg = big.tile([P, NB, BANK], BF16, name="hg", tag="big", align_bytes=64)
        hcodes = []
        hplane = []
        for j in range(NB):
            hc_t = const.tile([P, P], U32, name="hcodes_%d" % j, align_bytes=64)
            hp_t = const.tile([P, P], U8, name="hplane_%d" % j, align_bytes=64)
            hcodes.append(hc_t)
            hplane.append(hp_t)

        def h_value(j):
            tmp = work.tile([P, 4, P], F32, name="tmp", bufs=3)
            nc.vector.tensor_tensor(
                out=tmp[:], in0=ps1[j][:].rearrange("p (q t) -> p t q", t=4), in1=b1p[:, j, :, :], op=ALU.add
            )
            nc.scalar.activation(out=h_sb[:, j, :], in_=tmp[:].rearrange("p t q -> p (t q)"), func=ACT.Silu)

        def h_turn(j):
            ht = psum.tile([P, 4, P], BF16, name="ht", tag="ps")
            for t in range(4):
                nc.tensor.transpose(ht[:, t, :], h_sb[:, j, P * t : P * (t + 1)], ident_bf[:])
            dst = hg[:, j, :].rearrange("p (r t) -> p r t", t=4)
            src = ht[:].rearrange("p t r -> p r t")
            if j % 2 == 0:
                nc.vector.tensor_copy(out=dst, in_=src)
            else:
                nc.scalar.copy(out=dst, in_=src)

        def h_quant(j):
            nc.vector.quantize_mx(out=hcodes[j][:].bitcast(FP8X4), scales=hplane[j][:], in_=hg[:, j, :])

        for s in range(NB + 3):
            if s < NB:
                h_value(s)
            if 0 <= s - 2 < NB:
                h_turn(s - 2)
            if 0 <= s - 3 < NB:
                h_quant(s - 3)

        out_v = out.rearrange("b (n p) c -> (b n) (p c)", p=256)
        o_tiles = []
        g_start = []
        for ph in range(len(PHASES)):
            gs = 0 if ph == 0 else GAUSS_END[ph - 1]
            width = CH * (GAUSS_END[ph] - gs)
            o_t = opool.tile([P, LEAD + width], F32, name="o_%d" % ph, align_bytes=64)
            o_tiles.append(o_t[:, LEAD : LEAD + width].rearrange("p (n c) -> p n c", c=CH))
            g_start.append(gs)

        ss = const.tile([P, 256], F32, name="ss")
        rinv = const.tile([P, 256], F32, name="rinv")

        def matmuls_and_bias(ph):
            c0, c1 = PHASES[ph]
            banks = []
            lo = c0
            while lo < c1:
                hi = lo + max(n for n in (128, 256, BANK) if lo + n <= c1)
                banks.append((lo, hi))
                lo = hi
            acc = []
            for lo, hi in banks:
                acc_t = psum.tile([P, hi - lo], F32, name="acc_%d" % lo, tag="ps")
                acc.append(acc_t)
            for g in range(G2):
                planes = planes2a if g < 4 else planes2b
                k = 4 * (g % 4)
                for b, (lo, hi) in enumerate(banks):
                    nc.tensor.matmul_mx(
                        out=acc[b][:],
                        lhsT=hcodes[g][:].bitcast(FP8X4),
                        lhsT_scale=hplane[g][:],
                        rhs=w2[ph][g][:, lo - c0 : hi - c0].bitcast(FP8X4),
                        rhs_scale=planes[k:P, lo:hi],
                        start=(g == 0),
                        stop=(g == G2 - 1),
                    )
            cut = CH * GAUSS_END[ph]
            for b, (lo, hi) in enumerate(banks):
                pieces = [(lo, hi, ph)] if hi <= cut else [(lo, cut, ph), (cut, hi, ph + 1)]
                for a, e, tph in pieces:
                    off = CH * g_start[tph]
                    nc.vector.tensor_tensor(
                        out=o_tiles[tph].rearrange("p n c -> p (n c)")[:, a - off : e - off],
                        in0=acc[b][:, a - lo : e - lo],
                        in1=b2b[:, a:e],
                        op=ALU.add,
                    )

        def sigmoid(ph):
            o = o_tiles[ph]
            nc.scalar.activation(out=o[:, :, 0:7], in_=o[:, :, 0:7], func=ACT.Sigmoid)

        def square_sum_and_clip(ph):
            o = o_tiles[ph]
            sq = work.tile([P, GAUSS_END[ph] - g_start[ph], 4], F32, name="sq")
            nc.vector.tensor_tensor(out=sq[:], in0=o[:, :, 7:11], in1=o[:, :, 7:11], op=ALU.mult)
            nc.vector.tensor_reduce(out=ss[:, g_start[ph] : GAUSS_END[ph]], in_=sq[:], axis=AX.X, op=ALU.add)
            nc.vector.tensor_scalar(
                out=o[:, :, 11:14], in0=o[:, :, 11:14], scalar1=0.0, scalar2=1.0, op0=ALU.max, op1=ALU.min
            )

        def inverse_norm(first, last):
            cols = slice(g_start[first], GAUSS_END[last])
            nc.scalar.activation(out=rinv[:, cols], in_=ss[:, cols], func=ACT.Abs_reciprocal_sqrt)

        def means_and_sizes(ph):
            o = o_tiles[ph]
            nc.vector.scalar_tensor_tensor(
                out=o[:, :, 0:3],
                in0=o[:, :, 0:3],
                scalar=0.2,
                in1=xyz_f[:].unsqueeze(1).to_broadcast([P, GAUSS_END[ph] - g_start[ph], 3]),
                op0=ALU.mult,
                op1=ALU.add,
            )
            nc.vector.tensor_scalar(out=o[:, :, 4:7], in0=o[:, :, 4:7], scalar1=0.02, scalar2=None, op0=ALU.mult)

        def norm_and_store(ph):
            o = o_tiles[ph]
            n0, n1 = g_start[ph], GAUSS_END[ph]
            nc.vector.scalar_tensor_tensor(
                out=o[:, :, 7:11],
                in0=rinv[:, n0:n1].unsqueeze(2).to_broadcast([P, n1 - n0, 4]),
                scalar=1.0e12,
                in1=o[:, :, 7:11],
                op0=ALU.min,
                op1=ALU.mult,
            )
            nc.sync.dma_start(out=out_v[:, CH * n0 : CH * n1], in_=o.rearrange("p n c -> p (n c)"))

        matmuls_and_bias(0)
        sigmoid(0)
        square_sum_and_clip(0)
        inverse_norm(0, 0)
        means_and_sizes(0)

        matmuls_and_bias(1)
        sigmoid(1)
        square_sum_and_clip(1)
        inverse_norm(1, 1)
        norm_and_store(0)
        means_and_sizes(1)

        matmuls_and_bias(2)
        sigmoid(2)
        square_sum_and_clip(2)
        norm_and_store(1)

        matmuls_and_bias(3)
        sigmoid(3)
        square_sum_and_clip(3)
        inverse_norm(2, 3)
        means_and_sizes(2)
        means_and_sizes(3)
        norm_and_store(2)
        norm_and_store(3)
